import numpy as np
import ml_dtypes


def mxq(x, axis, fmt="e4m3"):
    dtype, down = {"e4m3": (ml_dtypes.float8_e4m3fn, 7), "e5m2": (ml_dtypes.float8_e5m2, 14)}[fmt]
    v = np.moveaxis(np.asarray(x, np.float32).astype(ml_dtypes.bfloat16).astype(np.float64), axis, -1)
    blocks = v.reshape(v.shape[:-1] + (-1, 32))
    amax = np.abs(blocks).max(-1, keepdims=True)
    byte = np.maximum(np.where(amax > 0, np.frexp(amax)[1] - 1 + 127, 0) - down, 1)
    scale = np.exp2(byte - 127.0)
    codes = (blocks / scale).astype(np.float32).astype(dtype).astype(np.float64)
    return np.moveaxis((codes * scale).reshape(v.shape), -1, axis)


WIDE = False


def mx_kscale(k):
    if not WIDE:
        return np.ones(k)
    levels = np.array([10, -10, 5, -5, 0])
    a = np.random.permutation(np.resize(levels, k // 512 * 4)).reshape(k // 512, 4)
    idx = np.arange(k)
    return np.exp2(a[idx // 512, idx % 128 // 32])


BF16 = ml_dtypes.bfloat16


def bf(x):
    return np.asarray(x, np.float32).astype(BF16)


def f64(x):
    return np.asarray(x).astype(np.float64)


B, S, DIM, N_HEADS, HEAD_DIM, F = 4, 2048, 512, 2, 64, 4096
QD = N_HEADS * HEAD_DIM
THETA = 10000.0
EPS = 1e-6


def rms_norm(x, w):
    return x * (1.0 / np.sqrt(np.mean(x * x, axis=-1, keepdims=True) + EPS)) * w


def rope_tables():
    inv = 1.0 / THETA ** (np.arange(0, HEAD_DIM, 2) / HEAD_DIM)
    freqs = np.outer(np.arange(S), inv)
    return np.cos(freqs), np.sin(freqs)


def rot(u, cos, sin):
    c = cos[None, :, None, :]
    s = sin[None, :, None, :]
    ur, ui = u[..., 0::2], u[..., 1::2]
    yr = ur * c - ui * s
    yi = ur * s + ui * c
    return np.stack([yr, yi], axis=-1).reshape(u.shape)


def setup_inputs():
    s = mx_kscale(DIM)
    sc = 1.0 / np.sqrt(DIM)
    quiet = np.where(np.random.random((B, S, 1)) < 0.125, 1e-3, 1.0)
    return {"x": bf(np.random.standard_normal((B, S, DIM)) * quiet),
            "attn_norm_w": bf((1.0 + 0.1 * np.random.standard_normal(DIM)) * s),
            "wq": bf(np.random.standard_normal((DIM, QD)) * sc / s[:, None]),
            "wk": bf(np.random.standard_normal((DIM, QD)) * sc / s[:, None]),
            "wv": bf(np.random.standard_normal((DIM, QD)) * sc / s[:, None])}


def reference(x, attn_norm_w, wq, wk, wv):
    h = rms_norm(f64(x), f64(attn_norm_w))
    hq = mxq(h, 2, "e4m3")
    q = (hq @ mxq(f64(wq), 0, "e4m3")).reshape(B, S, N_HEADS, HEAD_DIM)
    k = (hq @ mxq(f64(wk), 0, "e4m3")).reshape(B, S, N_HEADS, HEAD_DIM)
    v = (hq @ mxq(f64(wv), 0, "e4m3")).reshape(B, S, N_HEADS, HEAD_DIM)
    cos, sin = rope_tables()
    q = rot(q, cos, sin)
    k = rot(k, cos, sin)
    return q.transpose(0, 2, 1, 3), k.transpose(0, 2, 1, 3), v.transpose(0, 2, 1, 3)

@@ -1,0 +1,230 @@
+import math
+from contextlib import ExitStack
+
+import concourse.masks as masks
+import concourse.mybir as mybir
+
+F32 = mybir.dt.float32
+BF16 = mybir.dt.bfloat16
+U32 = mybir.dt.uint32
+U8 = mybir.dt.uint8
+FP8X4 = mybir.dt.float8_e4m3fn_x4
+ALU = mybir.AluOpType
+ACT = mybir.ActivationFunctionType
+
+P = 128
+BATCH, SEQ, DIM = 4, 2048, 512
+HEADS, HEAD_DIM = 2, 64
+QD = HEADS * HEAD_DIM
+PAIRS = HEAD_DIM // 2
+THETA = 10000.0
+EPS = 1e-6
+
+PACK = 4
+TILES = SEQ // P
+GROUP = 4
+GROUPS = TILES // GROUP
+ROT = 4 * QD
+W_COLS = ROT + QD
+
+ROUND_MAGIC = 1.5 * 2.0**23
+TURN_GRID = 2.0**15
+
+FLOPS = 2 * BATCH * SEQ * DIM * 3 * QD
+
+
+def build_rotation_table(nc, consts, work):
+    position = work.tile([P, TILES], F32)
+    nc.gpsimd.iota(
+        position[:], pattern=[[1, TILES]], base=0, channel_multiplier=TILES,
+        allow_small_or_imprecise_dtypes=True,
+    )
+    turns_hi = work.tile([P, TILES, PAIRS], F32)
+    turns_lo = work.tile([P, TILES, PAIRS], F32)
+    for j in range(PAIRS):
+        step = THETA ** (-j / PAIRS) / (2.0 * math.pi)
+        step_hi = round(step * TURN_GRID) / TURN_GRID
+        nc.vector.tensor_scalar_mul(out=turns_hi[:, :, j], in0=position[:], scalar1=step_hi)
+        nc.scalar.mul(out=turns_lo[:, :, j], in_=position[:], mul=step - step_hi)
+
+    whole = work.tile([P, TILES, PAIRS], F32)
+    nc.vector.tensor_scalar(
+        out=whole[:], in0=turns_hi[:], scalar1=ROUND_MAGIC, scalar2=ROUND_MAGIC,
+        op0=ALU.add, op1=ALU.subtract,
+    )
+    nc.vector.tensor_sub(out=turns_hi[:], in0=turns_hi[:], in1=whole[:])
+
+    turns = work.tile([P, TILES, 2, PAIRS], F32)
+    nc.vector.tensor_add(out=turns[:, :, 1, :], in0=turns_hi[:], in1=turns_lo[:])
+    nc.vector.tensor_scalar_add(out=turns[:, :, 0, :], in0=turns[:, :, 1, :], scalar1=0.25)
+    nearest = work.tile([P, TILES, 2, PAIRS], F32)
+    nc.vector.tensor_scalar(
+        out=nearest[:], in0=turns[:], scalar1=ROUND_MAGIC, scalar2=ROUND_MAGIC,
+        op0=ALU.add, op1=ALU.subtract,
+    )
+    nc.vector.tensor_sub(out=turns[:], in0=turns[:], in1=nearest[:])
+    trig = work.tile([P, TILES * 2 * PAIRS], F32)
+    nc.scalar.activation(
+        out=trig[:], in_=turns[:].rearrange("p i c j -> p (i c j)"), func=ACT.Sin,
+        scale=2.0 * math.pi,
+    )
+    table = consts.tile([P, TILES, 2, HEAD_DIM], F32)
+    nc.gpsimd.tensor_scalar(
+        out=table[:].rearrange("p i c (j r) -> p (i c j) r", r=2),
+        in0=trig[:].unsqueeze(2).to_broadcast([P, TILES * 2 * PAIRS, 2]),
+        scalar1=1.0, scalar2=0.0, op0=ALU.mult, op1=ALU.add,
+    )
+    return table
+
+
+def quantise_weights(nc, consts, work, wq, wk, wv):
+    raw = work.tile([P, 3, PACK, QD], BF16)
+    for m, w in enumerate((wq, wk, wv)):
+        nc.sync.dma_start(
+            out=raw[:, m].rearrange("p (u e) c -> p u (e c)", u=2),
+            in_=w.rearrange("(u p e) c -> p u (e c)", u=2, e=2),
+        )
+    grouped = work.tile([P, W_COLS, PACK], BF16, align_bytes=64)
+    nc.vector.tensor_copy(
+        out=grouped[:, 0 : 2 * QD, :].rearrange("p (m c) t -> p m c t", m=2),
+        in_=raw[:, 0:2].rearrange("p m t c -> p m c t"),
+    )
+    partner = grouped[:, 2 * QD : ROT, :].rearrange("p (m j r) t -> p m j r t", m=2, r=2)
+    pairs = raw[:, 0:2].rearrange("p m t (j r) -> p m j r t", r=2)
+    nc.vector.tensor_scalar_mul(out=partner[:, :, :, 0, :], in0=pairs[:, :, :, 1, :], scalar1=-1.0)
+    nc.vector.tensor_copy(out=partner[:, :, :, 1, :], in_=pairs[:, :, :, 0, :])
+    nc.vector.tensor_copy(out=grouped[:, ROT:W_COLS, :], in_=raw[:, 2].rearrange("p t c -> p c t"))
+
+    codes = consts.tile([P, W_COLS], U32, align_bytes=64)
+    scales = consts.tile([P, W_COLS], U8, align_bytes=64)
+    for cols in (slice(0, ROT), slice(ROT, W_COLS)):
+        nc.vector.quantize_mx(
+            out=codes[:, cols].bitcast(FP8X4),
+            scales=scales[:, cols],
+            in_=grouped[:, cols, :].rearrange("p c t -> p (c t)"),
+        )
+    return codes, scales
+
+
+def tile_flexattentionblock_pa_t_kernel(tc, x, attn_norm_w, wq, wk, wv, out_0, out_1, out_2):
+    nc = tc.nc
+    with ExitStack() as ctx:
+        consts = ctx.enter_context(tc.tile_pool(name="consts", bufs=1))
+        setup = ctx.enter_context(tc.tile_pool(name="setup", bufs=1))
+        resident = ctx.enter_context(tc.tile_pool(name="resident", bufs=1))
+        stream = ctx.enter_context(tc.tile_pool(name="stream", bufs=3))
+        psum_gain = ctx.enter_context(tc.psum_pool(name="psum_gain", bufs=1))
+        psum_t = ctx.enter_context(tc.psum_pool(name="psum_t", bufs=2))
+        psum_rot = ctx.enter_context(tc.psum_pool(name="psum_rot", bufs=4))
+        psum_v = ctx.enter_context(tc.psum_pool(name="psum_v", bufs=1))
+
+        zero_col = setup.tile([P, 1], F32)
+        nc.vector.memset(zero_col[:], 0.0)
+        nc.scalar.activation(out=zero_col[:], in_=zero_col[:], func=ACT.Sin)
+
+        gain_row = setup.tile([P, DIM], BF16)
+        nc.vector.memset(gain_row[:], 0.0)
+        x_groups = []
+        for b in range(BATCH):
+            tokens = x[b].rearrange("(p i) k -> p i k", i=TILES)
+            for g in range(GROUPS):
+                x_sb = resident.tile([P, GROUP, DIM], BF16, name="x_%d_%d" % (b, g))
+                nc.sync.dma_start(out=x_sb[:], in_=tokens[:, g * GROUP : (g + 1) * GROUP, :])
+                x_groups.append(x_sb)
+                if b == 0 and g == 0:
+                    nc.sync.dma_start(
+                        out=gain_row[0:1, :], in_=attn_norm_w.rearrange("(o k) -> o k", o=1)
+                    )
+                    w_codes, w_scales = quantise_weights(nc, consts, setup, wq, wk, wv)
+
+        ones = setup.tile([P, P], BF16)
+        nc.vector.memset(ones[:], 1.0)
+        gain = psum_gain.tile([P, DIM], F32)
+        nc.tensor.matmul(out=gain[:], lhsT=ones[:], rhs=gain_row[:], start=True, stop=True)
+
+        identity = consts.tile([P, P], F32)
+        masks.make_identity(nc, identity[:])
+        minus_half = consts.tile([P, GROUP], F32)
+        nc.gpsimd.memset(minus_half[:], -0.5)
+        table = build_rotation_table(nc, consts, setup)
+
+        for n, x_sb in enumerate(x_groups):
+            b, g = divmod(n, GROUPS)
+
+            squares = stream.tile([P, GROUP], F32)
+            for t in range(GROUP):
+                unread = stream.tile([P, DIM], BF16)
+                nc.scalar.activation(
+                    out=unread[:], in_=x_sb[:, t, :], func=ACT.Square,
+                    accum_out=squares[:, t : t + 1],
+                )
+            mean_sq = stream.tile([P, GROUP], F32)
+            nc.gpsimd.tensor_scalar(
+                out=mean_sq[:], in0=squares[:], scalar1=1.0 / DIM, scalar2=EPS,
+                op0=ALU.mult, op1=ALU.add,
+            )
+            rstd = stream.tile([P, GROUP], F32)
+            nc.gpsimd.tensor_tensor(out=rstd[:], in0=mean_sq[:], in1=minus_half[:], op=ALU.pow)
+
+            h = stream.tile([P, GROUP, DIM], BF16)
+            for t in range(GROUP):
+                nc.vector.scalar_tensor_tensor(
+                    out=h[:, t, :], in0=x_sb[:, t, :], scalar=rstd[:, t : t + 1], in1=gain[:],
+                    op0=ALU.mult, op1=ALU.mult,
+                )
+
+            grouped = stream.tile([P, GROUP * P * PACK], BF16, align_bytes=64)
+            grouped_words = grouped[:].bitcast(F32).rearrange("p (r u) -> p r u", u=2)
+            for half in range(GROUP // 2):
+                turned = psum_t.tile([P, 2, 2 * P], F32)
+                for s in range(2):
+                    words = h[:, 2 * half + s, :].bitcast(F32)
+                    for u in range(2):
+                        nc.tensor.transpose(
+                            out=turned[:, u, s * P : (s + 1) * P],
+                            in_=words[:, u * P : (u + 1) * P],
+                            identity=identity[:],
+                        )
+                nc.scalar.copy(
+                    out=grouped_words[:, half * 2 * P : (half + 1) * 2 * P, :],
+                    in_=turned[:].rearrange("p u r -> p r u"),
+                )
+            h_codes = stream.tile([P, GROUP * P], U32, align_bytes=64)
+            h_scales = stream.tile([P, GROUP * P], U8, align_bytes=64)
+            nc.vector.quantize_mx(out=h_codes[:].bitcast(FP8X4), scales=h_scales[:], in_=grouped[:])
+
+            rotated = stream.tile([P, 2 * HEADS, GROUP, HEAD_DIM], F32)
+            v_ps = psum_v.tile([P, GROUP, QD], F32)
+            for t in range(GROUP):
+                cols = slice(t * P, (t + 1) * P)
+                rot_ps = psum_rot.tile([P, ROT], F32)
+                nc.tensor.matmul_mx(
+                    out=rot_ps[:],
+                    lhsT=h_codes[:, cols].bitcast(FP8X4), lhsT_scale=h_scales[:, cols],
+                    rhs=w_codes[:, 0:ROT].bitcast(FP8X4), rhs_scale=w_scales[:, 0:ROT],
+                    start=True, stop=True,
+                )
+                nc.tensor.matmul_mx(
+                    out=v_ps[:, t, :],
+                    lhsT=h_codes[:, cols].bitcast(FP8X4), lhsT_scale=h_scales[:, cols],
+                    rhs=w_codes[:, ROT:W_COLS].bitcast(FP8X4), rhs_scale=w_scales[:, ROT:W_COLS],
+                    start=True, stop=True,
+                )
+                products = stream.tile([P, 2, 2 * HEADS, HEAD_DIM], F32)
+                nc.vector.tensor_tensor(
+                    out=products[:],
+                    in0=rot_ps[:].rearrange("p (c r d) -> p c r d", c=2, r=2 * HEADS),
+                    in1=table[:, g * GROUP + t].unsqueeze(2).to_broadcast([P, 2, 2 * HEADS, HEAD_DIM]),
+                    op=ALU.mult,
+                )
+                nc.gpsimd.tensor_tensor(
+                    out=rotated[:, :, t, :], in0=products[:, 0], in1=products[:, 1], op=ALU.add
+                )
+            v_sb = stream.tile([P, HEADS, GROUP, HEAD_DIM], F32)
+            nc.scalar.copy(out=v_sb[:], in_=v_ps[:].rearrange("p t (h d) -> p h t d", h=HEADS))
+
+            span = slice(g * GROUP, (g + 1) * GROUP)
+            for dram, sb in ((out_0, rotated[:, 0:HEADS]), (out_1, rotated[:, HEADS:]), (out_2, v_sb[:])):
+                nc.sync.dma_start(
+                    out=dram[b].rearrange("h (p i) d -> p h i d", i=TILES)[:, :, span, :], in_=sb
+                )

@@ -33,7 +33,7 @@ TURN_GRID = 2.0**15
 FLOPS = 2 * BATCH * SEQ * DIM * 3 * QD
 
 
-def build_rotation_table(nc, consts, work):
+def rotation_turns(nc, work):
     position = work.tile([P, TILES], F32)
     nc.gpsimd.iota(
         position[:], pattern=[[1, TILES]], base=0, channel_multiplier=TILES,
@@ -63,6 +63,10 @@ def build_rotation_table(nc, consts, work):
         op0=ALU.add, op1=ALU.subtract,
     )
     nc.vector.tensor_sub(out=turns[:], in0=turns[:], in1=nearest[:])
+    return turns
+
+
+def rotation_table(nc, consts, work, turns):
     trig = work.tile([P, TILES * 2 * PAIRS], F32)
     nc.scalar.activation(
         out=trig[:], in_=turns[:].rearrange("p i c j -> p (i c j)"), func=ACT.Sin,
@@ -77,13 +81,17 @@ def build_rotation_table(nc, consts, work):
     return table
 
 
-def quantise_weights(nc, consts, work, wq, wk, wv):
+def load_weights(nc, work, wq, wk, wv):
     raw = work.tile([P, 3, PACK, QD], BF16)
     for m, w in enumerate((wq, wk, wv)):
         nc.sync.dma_start(
             out=raw[:, m].rearrange("p (u e) c -> p u (e c)", u=2),
             in_=w.rearrange("(u p e) c -> p u (e c)", u=2, e=2),
         )
+    return raw
+
+
+def quantise_weights(nc, consts, work, raw):
     grouped = work.tile([P, W_COLS, PACK], BF16, align_bytes=64)
     nc.vector.tensor_copy(
         out=grouped[:, 0 : 2 * QD, :].rearrange("p (m c) t -> p m c t", m=2),
@@ -108,15 +116,18 @@ def quantise_weights(nc, consts, work, wq, wk, wv):
 
 def tile_flexattentionblock_pa_t_kernel(tc, x, attn_norm_w, wq, wk, wv, out_0, out_1, out_2):
     nc = tc.nc
+    n_groups = BATCH * GROUPS
     with ExitStack() as ctx:
         consts = ctx.enter_context(tc.tile_pool(name="consts", bufs=1))
         setup = ctx.enter_context(tc.tile_pool(name="setup", bufs=1))
         resident = ctx.enter_context(tc.tile_pool(name="resident", bufs=1))
         stream = ctx.enter_context(tc.tile_pool(name="stream", bufs=3))
+        per_tile = ctx.enter_context(tc.tile_pool(name="per_tile", bufs=GROUP))
         psum_gain = ctx.enter_context(tc.psum_pool(name="psum_gain", bufs=1))
         psum_t = ctx.enter_context(tc.psum_pool(name="psum_t", bufs=2))
-        psum_rot = ctx.enter_context(tc.psum_pool(name="psum_rot", bufs=4))
+        psum_rot = ctx.enter_context(tc.psum_pool(name="psum_rot", bufs=GROUP))
         psum_v = ctx.enter_context(tc.psum_pool(name="psum_v", bufs=1))
+        ctx.enter_context(tc.manual_schedule())
 
         zero_col = setup.tile([P, 1], F32)
         nc.vector.memset(zero_col[:], 0.0)
@@ -135,66 +146,81 @@ def tile_flexattentionblock_pa_t_kernel(tc, x, attn_norm_w, wq, wk, wv, out_0, o
                     nc.sync.dma_start(
                         out=gain_row[0:1, :], in_=attn_norm_w.rearrange("(o k) -> o k", o=1)
                     )
-                    w_codes, w_scales = quantise_weights(nc, consts, setup, wq, wk, wv)
+                    w_raw = load_weights(nc, setup, wq, wk, wv)
+
+        turns = rotation_turns(nc, setup)
+        identity = consts.tile([P, P], F32)
+        masks.make_identity(nc, identity[:])
+        minus_half = consts.tile([P, GROUP], F32)
+        nc.gpsimd.memset(minus_half[:], -0.5)
 
         ones = setup.tile([P, P], BF16)
         nc.vector.memset(ones[:], 1.0)
         gain = psum_gain.tile([P, DIM], F32)
         nc.tensor.matmul(out=gain[:], lhsT=ones[:], rhs=gain_row[:], start=True, stop=True)
+        w_codes, w_scales = quantise_weights(nc, consts, setup, w_raw)
 
-        identity = consts.tile([P, P], F32)
-        masks.make_identity(nc, identity[:])
-        minus_half = consts.tile([P, GROUP], F32)
-        nc.gpsimd.memset(minus_half[:], -0.5)
-        table = build_rotation_table(nc, consts, setup)
+        squares_of, rstd_of, h_of, grouped_of, codes_of, banks_of = {}, {}, {}, {}, {}, {}
 
-        for n, x_sb in enumerate(x_groups):
-            b, g = divmod(n, GROUPS)
-
-            squares = stream.tile([P, GROUP], F32)
-            for t in range(GROUP):
-                unread = stream.tile([P, DIM], BF16)
+        def sum_squares(n, half):
+            if half == 0:
+                squares = stream.tile([P, GROUP], F32)
+                squares_of[n] = squares
+            for t in (2 * half, 2 * half + 1):
+                unread = per_tile.tile([P, DIM], BF16)
                 nc.scalar.activation(
-                    out=unread[:], in_=x_sb[:, t, :], func=ACT.Square,
-                    accum_out=squares[:, t : t + 1],
+                    out=unread[:], in_=x_groups[n][:, t, :], func=ACT.Square,
+                    accum_out=squares_of[n][:, t : t + 1],
                 )
+
+        def finish_rstd(n):
             mean_sq = stream.tile([P, GROUP], F32)
             nc.gpsimd.tensor_scalar(
-                out=mean_sq[:], in0=squares[:], scalar1=1.0 / DIM, scalar2=EPS,
+                out=mean_sq[:], in0=squares_of[n][:], scalar1=1.0 / DIM, scalar2=EPS,
                 op0=ALU.mult, op1=ALU.add,
             )
             rstd = stream.tile([P, GROUP], F32)
             nc.gpsimd.tensor_tensor(out=rstd[:], in0=mean_sq[:], in1=minus_half[:], op=ALU.pow)
+            rstd_of[n] = rstd
 
-            h = stream.tile([P, GROUP, DIM], BF16)
-            for t in range(GROUP):
+        def scale_and_turn(n, half):
+            if half == 0:
+                h = stream.tile([P, GROUP, DIM], BF16)
+                grouped = stream.tile([P, GROUP * P * PACK], BF16, align_bytes=64)
+                h_of[n], grouped_of[n] = h, grouped
+            h = h_of[n]
+            for t in (2 * half, 2 * half + 1):
                 nc.vector.scalar_tensor_tensor(
-                    out=h[:, t, :], in0=x_sb[:, t, :], scalar=rstd[:, t : t + 1], in1=gain[:],
-                    op0=ALU.mult, op1=ALU.mult,
+                    out=h[:, t, :], in0=x_groups[n][:, t, :], scalar=rstd_of[n][:, t : t + 1],
+                    in1=gain[:], op0=ALU.mult, op1=ALU.mult,
                 )
+            turned = psum_t.tile([P, 2, 2 * P], F32)
+            for s in range(2):
+                words = h[:, 2 * half + s, :].bitcast(F32)
+                for u in range(2):
+                    nc.tensor.transpose(
+                        out=turned[:, u, s * P : (s + 1) * P],
+                        in_=words[:, u * P : (u + 1) * P],
+                        identity=identity[:],
+                    )
+            grouped_words = grouped_of[n][:].bitcast(F32).rearrange("p (r u) -> p r u", u=2)
+            nc.scalar.copy(
+                out=grouped_words[:, half * 2 * P : (half + 1) * 2 * P, :],
+                in_=turned[:].rearrange("p u r -> p r u"),
+            )
 
-            grouped = stream.tile([P, GROUP * P * PACK], BF16, align_bytes=64)
-            grouped_words = grouped[:].bitcast(F32).rearrange("p (r u) -> p r u", u=2)
-            for half in range(GROUP // 2):
-                turned = psum_t.tile([P, 2, 2 * P], F32)
-                for s in range(2):
-                    words = h[:, 2 * half + s, :].bitcast(F32)
-                    for u in range(2):
-                        nc.tensor.transpose(
-                            out=turned[:, u, s * P : (s + 1) * P],
-                            in_=words[:, u * P : (u + 1) * P],
-                            identity=identity[:],
-                        )
-                nc.scalar.copy(
-                    out=grouped_words[:, half * 2 * P : (half + 1) * 2 * P, :],
-                    in_=turned[:].rearrange("p u r -> p r u"),
-                )
+        def quantise(n):
             h_codes = stream.tile([P, GROUP * P], U32, align_bytes=64)
             h_scales = stream.tile([P, GROUP * P], U8, align_bytes=64)
-            nc.vector.quantize_mx(out=h_codes[:].bitcast(FP8X4), scales=h_scales[:], in_=grouped[:])
+            nc.vector.quantize_mx(
+                out=h_codes[:].bitcast(FP8X4), scales=h_scales[:], in_=grouped_of[n][:]
+            )
+            codes_of[n] = (h_codes, h_scales)
 
-            rotated = stream.tile([P, 2 * HEADS, GROUP, HEAD_DIM], F32)
+        def project(n):
+            h_codes, h_scales = codes_of[n]
             v_ps = psum_v.tile([P, GROUP, QD], F32)
+            rot_banks = []
             for t in range(GROUP):
                 cols = slice(t * P, (t + 1) * P)
                 rot_ps = psum_rot.tile([P, ROT], F32)
@@ -210,21 +236,62 @@ def tile_flexattentionblock_pa_t_kernel(tc, x, attn_norm_w, wq, wk, wv, out_0, o
                     rhs=w_codes[:, ROT:W_COLS].bitcast(FP8X4), rhs_scale=w_scales[:, ROT:W_COLS],
                     start=True, stop=True,
                 )
-                products = stream.tile([P, 2, 2 * HEADS, HEAD_DIM], F32)
+                rot_banks.append(rot_ps)
+            banks_of[n] = (rot_banks, v_ps)
+
+        def store(n, dram, sb):
+            b, g = divmod(n, GROUPS)
+            rows = dram[b].rearrange("h (p i) d -> p h i d", i=TILES)
+            nc.sync.dma_start(out=rows[:, :, g * GROUP : (g + 1) * GROUP, :], in_=sb)
+
+        def store_v(n):
+            v_sb = stream.tile([P, HEADS, GROUP, HEAD_DIM], F32)
+            nc.scalar.copy(
+                out=v_sb[:], in_=banks_of[n][1][:].rearrange("p t (h d) -> p h t d", h=HEADS)
+            )
+            store(n, out_2, v_sb[:])
+
+        def rotate_and_store(n):
+            first_tile = (n % GROUPS) * GROUP
+            rotated = stream.tile([P, 2 * HEADS, GROUP, HEAD_DIM], F32)
+            for t in range(GROUP):
+                products = per_tile.tile([P, 2, 2 * HEADS, HEAD_DIM], F32)
                 nc.vector.tensor_tensor(
                     out=products[:],
-                    in0=rot_ps[:].rearrange("p (c r d) -> p c r d", c=2, r=2 * HEADS),
-                    in1=table[:, g * GROUP + t].unsqueeze(2).to_broadcast([P, 2, 2 * HEADS, HEAD_DIM]),
+                    in0=banks_of[n][0][t][:].rearrange("p (c r d) -> p c r d", c=2, r=2 * HEADS),
+                    in1=table[:, first_tile + t].unsqueeze(2).to_broadcast(
+                        [P, 2, 2 * HEADS, HEAD_DIM]
+                    ),
                     op=ALU.mult,
                 )
                 nc.gpsimd.tensor_tensor(
                     out=rotated[:, :, t, :], in0=products[:, 0], in1=products[:, 1], op=ALU.add
                 )
-            v_sb = stream.tile([P, HEADS, GROUP, HEAD_DIM], F32)
-            nc.scalar.copy(out=v_sb[:], in_=v_ps[:].rearrange("p t (h d) -> p h t d", h=HEADS))
+            store(n, out_0, rotated[:, 0:HEADS])
+            store(n, out_1, rotated[:, HEADS:])
 
-            span = slice(g * GROUP, (g + 1) * GROUP)
-            for dram, sb in ((out_0, rotated[:, 0:HEADS]), (out_1, rotated[:, HEADS:]), (out_2, v_sb[:])):
-                nc.sync.dma_start(
-                    out=dram[b].rearrange("h (p i) d -> p h i d", i=TILES)[:, :, span, :], in_=sb
-                )
+        for n in range(2):
+            sum_squares(n, 0)
+            sum_squares(n, 1)
+            finish_rstd(n)
+        table = rotation_table(nc, consts, setup, turns)
+
+        for n in range(n_groups + 1):
+            ahead, behind = n + 2, n - 1
+            if ahead < n_groups:
+                sum_squares(ahead, 0)
+            if n < n_groups:
+                scale_and_turn(n, 0)
+            if behind >= 0:
+                quantise(behind)
+            if ahead < n_groups:
+                sum_squares(ahead, 1)
+            if behind >= 0:
+                project(behind)
+                store_v(behind)
+            if n < n_groups:
+                scale_and_turn(n, 1)
+            if behind >= 0:
+                rotate_and_store(behind)
+            if ahead < n_groups:
+                finish_rstd(ahead)

@@ -160,7 +160,8 @@ def tile_flexattentionblock_pa_t_kernel(tc, x, attn_norm_w, wq, wk, wv, out_0, o
         nc.tensor.matmul(out=gain[:], lhsT=ones[:], rhs=gain_row[:], start=True, stop=True)
         w_codes, w_scales = quantise_weights(nc, consts, setup, w_raw)
 
-        squares_of, rstd_of, h_of, grouped_of, codes_of, banks_of = {}, {}, {}, {}, {}, {}
+        squares_of, rstd_of, h_of, grouped_of, codes_of = {}, {}, {}, {}, {}
+        v_bank_of, rot_banks_of = {}, {}
 
         def sum_squares(n, half):
             if half == 0:
@@ -217,9 +218,21 @@ def tile_flexattentionblock_pa_t_kernel(tc, x, attn_norm_w, wq, wk, wv, out_0, o
             )
             codes_of[n] = (h_codes, h_scales)
 
-        def project(n):
+        def project_v(n):
             h_codes, h_scales = codes_of[n]
             v_ps = psum_v.tile([P, GROUP, QD], F32)
+            for t in range(GROUP):
+                cols = slice(t * P, (t + 1) * P)
+                nc.tensor.matmul_mx(
+                    out=v_ps[:, t, :],
+                    lhsT=h_codes[:, cols].bitcast(FP8X4), lhsT_scale=h_scales[:, cols],
+                    rhs=w_codes[:, ROT:W_COLS].bitcast(FP8X4), rhs_scale=w_scales[:, ROT:W_COLS],
+                    start=True, stop=True,
+                )
+            v_bank_of[n] = v_ps
+
+        def project_rot(n):
+            h_codes, h_scales = codes_of[n]
             rot_banks = []
             for t in range(GROUP):
                 cols = slice(t * P, (t + 1) * P)
@@ -230,14 +243,8 @@ def tile_flexattentionblock_pa_t_kernel(tc, x, attn_norm_w, wq, wk, wv, out_0, o
                     rhs=w_codes[:, 0:ROT].bitcast(FP8X4), rhs_scale=w_scales[:, 0:ROT],
                     start=True, stop=True,
                 )
-                nc.tensor.matmul_mx(
-                    out=v_ps[:, t, :],
-                    lhsT=h_codes[:, cols].bitcast(FP8X4), lhsT_scale=h_scales[:, cols],
-                    rhs=w_codes[:, ROT:W_COLS].bitcast(FP8X4), rhs_scale=w_scales[:, ROT:W_COLS],
-                    start=True, stop=True,
-                )
                 rot_banks.append(rot_ps)
-            banks_of[n] = (rot_banks, v_ps)
+            rot_banks_of[n] = rot_banks
 
         def store(n, dram, sb):
             b, g = divmod(n, GROUPS)
@@ -247,7 +254,7 @@ def tile_flexattentionblock_pa_t_kernel(tc, x, attn_norm_w, wq, wk, wv, out_0, o
         def store_v(n):
             v_sb = stream.tile([P, HEADS, GROUP, HEAD_DIM], F32)
             nc.scalar.copy(
-                out=v_sb[:], in_=banks_of[n][1][:].rearrange("p t (h d) -> p h t d", h=HEADS)
+                out=v_sb[:], in_=v_bank_of[n][:].rearrange("p t (h d) -> p h t d", h=HEADS)
             )
             store(n, out_2, v_sb[:])
 
@@ -258,7 +265,7 @@ def tile_flexattentionblock_pa_t_kernel(tc, x, attn_norm_w, wq, wk, wv, out_0, o
                 products = per_tile.tile([P, 2, 2 * HEADS, HEAD_DIM], F32)
                 nc.vector.tensor_tensor(
                     out=products[:],
-                    in0=banks_of[n][0][t][:].rearrange("p (c r d) -> p c r d", c=2, r=2 * HEADS),
+                    in0=rot_banks_of[n][t][:].rearrange("p (c r d) -> p c r d", c=2, r=2 * HEADS),
                     in1=table[:, first_tile + t].unsqueeze(2).to_broadcast(
                         [P, 2, 2 * HEADS, HEAD_DIM]
                     ),
@@ -276,22 +283,24 @@ def tile_flexattentionblock_pa_t_kernel(tc, x, attn_norm_w, wq, wk, wv, out_0, o
             finish_rstd(n)
         table = rotation_table(nc, consts, setup, turns)
 
-        for n in range(n_groups + 1):
-            ahead, behind = n + 2, n - 1
+        for n in range(n_groups + 2):
+            ahead, behind, last = n + 2, n - 1, n - 2
             if ahead < n_groups:
                 sum_squares(ahead, 0)
             if n < n_groups:
                 scale_and_turn(n, 0)
-            if behind >= 0:
+            if 0 <= behind < n_groups:
                 quantise(behind)
             if ahead < n_groups:
                 sum_squares(ahead, 1)
-            if behind >= 0:
-                project(behind)
-                store_v(behind)
             if n < n_groups:
                 scale_and_turn(n, 1)
-            if behind >= 0:
-                rotate_and_store(behind)
+            if 0 <= behind < n_groups:
+                project_v(behind)
+                store_v(behind)
+            if last >= 0:
+                rotate_and_store(last)
+            if 0 <= behind < n_groups:
+                project_rot(behind)
             if ahead < n_groups:
                 finish_rstd(ahead)

@@ -151,8 +151,8 @@ def tile_flexattentionblock_pa_t_kernel(tc, x, attn_norm_w, wq, wk, wv, out_0, o
         turns = rotation_turns(nc, setup)
         identity = consts.tile([P, P], F32)
         masks.make_identity(nc, identity[:])
-        minus_half = consts.tile([P, GROUP], F32)
-        nc.gpsimd.memset(minus_half[:], -0.5)
+        eps_col = consts.tile([P, 1], F32)
+        nc.vector.memset(eps_col[:], EPS)
 
         ones = setup.tile([P, P], BF16)
         nc.vector.memset(ones[:], 1.0)
@@ -160,7 +160,7 @@ def tile_flexattentionblock_pa_t_kernel(tc, x, attn_norm_w, wq, wk, wv, out_0, o
         nc.tensor.matmul(out=gain[:], lhsT=ones[:], rhs=gain_row[:], start=True, stop=True)
         w_codes, w_scales = quantise_weights(nc, consts, setup, w_raw)
 
-        squares_of, rstd_of, h_of, grouped_of, codes_of = {}, {}, {}, {}, {}
+        squares_of, root_of, rstd_of, h_of, grouped_of, codes_of = {}, {}, {}, {}, {}, {}
         v_bank_of, rot_banks_of = {}, {}
 
         def sum_squares(n, half):
@@ -174,14 +174,16 @@ def tile_flexattentionblock_pa_t_kernel(tc, x, attn_norm_w, wq, wk, wv, out_0, o
                     accum_out=squares_of[n][:, t : t + 1],
                 )
 
-        def finish_rstd(n):
-            mean_sq = stream.tile([P, GROUP], F32)
-            nc.gpsimd.tensor_scalar(
-                out=mean_sq[:], in0=squares_of[n][:], scalar1=1.0 / DIM, scalar2=EPS,
-                op0=ALU.mult, op1=ALU.add,
+        def root_mean_square(n):
+            root = stream.tile([P, GROUP], F32)
+            nc.scalar.activation(
+                out=root[:], in_=squares_of[n][:], func=ACT.Sqrt, scale=1.0 / DIM, bias=eps_col[:]
             )
+            root_of[n] = root
+
+        def reciprocal_root(n):
             rstd = stream.tile([P, GROUP], F32)
-            nc.gpsimd.tensor_tensor(out=rstd[:], in0=mean_sq[:], in1=minus_half[:], op=ALU.pow)
+            nc.vector.reciprocal(out=rstd[:], in_=root_of[n][:])
             rstd_of[n] = rstd
 
         def scale_and_turn(n, half):
@@ -277,11 +279,14 @@ def tile_flexattentionblock_pa_t_kernel(tc, x, attn_norm_w, wq, wk, wv, out_0, o
             store(n, out_0, rotated[:, 0:HEADS])
             store(n, out_1, rotated[:, HEADS:])
 
-        for n in range(2):
-            sum_squares(n, 0)
-            sum_squares(n, 1)
-            finish_rstd(n)
+        sum_squares(0, 0)
+        sum_squares(0, 1)
         table = rotation_table(nc, consts, setup, turns)
+        root_mean_square(0)
+        reciprocal_root(0)
+        sum_squares(1, 0)
+        sum_squares(1, 1)
+        root_mean_square(1)
 
         for n in range(n_groups + 2):
             ahead, behind, last = n + 2, n - 1, n - 2
@@ -293,8 +298,11 @@ def tile_flexattentionblock_pa_t_kernel(tc, x, attn_norm_w, wq, wk, wv, out_0, o
                 quantise(behind)
             if ahead < n_groups:
                 sum_squares(ahead, 1)
+                root_mean_square(ahead)
             if n < n_groups:
                 scale_and_turn(n, 1)
+            if n + 1 < n_groups:
+                reciprocal_root(n + 1)
             if 0 <= behind < n_groups:
                 project_v(behind)
                 store_v(behind)
@@ -302,5 +310,3 @@ def tile_flexattentionblock_pa_t_kernel(tc, x, attn_norm_w, wq, wk, wv, out_0, o
                 rotate_and_store(last)
             if 0 <= behind < n_groups:
                 project_rot(behind)
-            if ahead < n_groups:
-                finish_rstd(ahead)

import math
from contextlib import ExitStack

import concourse.masks as masks
import concourse.mybir as mybir

F32 = mybir.dt.float32
BF16 = mybir.dt.bfloat16
U32 = mybir.dt.uint32
U8 = mybir.dt.uint8
FP8X4 = mybir.dt.float8_e4m3fn_x4
ALU = mybir.AluOpType
ACT = mybir.ActivationFunctionType

P = 128
BATCH, SEQ, DIM = 4, 2048, 512
HEADS, HEAD_DIM = 2, 64
QD = HEADS * HEAD_DIM
PAIRS = HEAD_DIM // 2
THETA = 10000.0
EPS = 1e-6

PACK = 4
TILES = SEQ // P
GROUP = 4
GROUPS = TILES // GROUP
ROT = 4 * QD
W_COLS = ROT + QD

ROUND_MAGIC = 1.5 * 2.0**23
TURN_GRID = 2.0**15

FLOPS = 2 * BATCH * SEQ * DIM * 3 * QD


def rotation_turns(nc, work):
    position = work.tile([P, TILES], F32)
    nc.gpsimd.iota(
        position[:], pattern=[[1, TILES]], base=0, channel_multiplier=TILES,
        allow_small_or_imprecise_dtypes=True,
    )
    turns_hi = work.tile([P, TILES, PAIRS], F32)
    turns_lo = work.tile([P, TILES, PAIRS], F32)
    for j in range(PAIRS):
        step = THETA ** (-j / PAIRS) / (2.0 * math.pi)
        step_hi = round(step * TURN_GRID) / TURN_GRID
        nc.vector.tensor_scalar_mul(out=turns_hi[:, :, j], in0=position[:], scalar1=step_hi)
        nc.scalar.mul(out=turns_lo[:, :, j], in_=position[:], mul=step - step_hi)

    whole = work.tile([P, TILES, PAIRS], F32)
    nc.vector.tensor_scalar(
        out=whole[:], in0=turns_hi[:], scalar1=ROUND_MAGIC, scalar2=ROUND_MAGIC,
        op0=ALU.add, op1=ALU.subtract,
    )
    nc.vector.tensor_sub(out=turns_hi[:], in0=turns_hi[:], in1=whole[:])

    turns = work.tile([P, TILES, 2, PAIRS], F32)
    nc.vector.tensor_add(out=turns[:, :, 1, :], in0=turns_hi[:], in1=turns_lo[:])
    nc.vector.tensor_scalar_add(out=turns[:, :, 0, :], in0=turns[:, :, 1, :], scalar1=0.25)
    nearest = work.tile([P, TILES, 2, PAIRS], F32)
    nc.vector.tensor_scalar(
        out=nearest[:], in0=turns[:], scalar1=ROUND_MAGIC, scalar2=ROUND_MAGIC,
        op0=ALU.add, op1=ALU.subtract,
    )
    nc.vector.tensor_sub(out=turns[:], in0=turns[:], in1=nearest[:])
    return turns


def rotation_table(nc, consts, work, turns):
    trig = work.tile([P, TILES * 2 * PAIRS], F32)
    nc.scalar.activation(
        out=trig[:], in_=turns[:].rearrange("p i c j -> p (i c j)"), func=ACT.Sin,
        scale=2.0 * math.pi,
    )
    table = consts.tile([P, TILES, 2, HEAD_DIM], F32)
    nc.gpsimd.tensor_scalar(
        out=table[:].rearrange("p i c (j r) -> p (i c j) r", r=2),
        in0=trig[:].unsqueeze(2).to_broadcast([P, TILES * 2 * PAIRS, 2]),
        scalar1=1.0, scalar2=0.0, op0=ALU.mult, op1=ALU.add,
    )
    return table


def load_weights(nc, work, wq, wk, wv):
    raw = work.tile([P, 3, PACK, QD], BF16)
    for m, w in enumerate((wq, wk, wv)):
        nc.sync.dma_start(
            out=raw[:, m].rearrange("p (u e) c -> p u (e c)", u=2),
            in_=w.rearrange("(u p e) c -> p u (e c)", u=2, e=2),
        )
    return raw


def quantise_weights(nc, consts, work, raw):
    grouped = work.tile([P, W_COLS, PACK], BF16, align_bytes=64)
    nc.vector.tensor_copy(
        out=grouped[:, 0 : 2 * QD, :].rearrange("p (m c) t -> p m c t", m=2),
        in_=raw[:, 0:2].rearrange("p m t c -> p m c t"),
    )
    partner = grouped[:, 2 * QD : ROT, :].rearrange("p (m j r) t -> p m j r t", m=2, r=2)
    pairs = raw[:, 0:2].rearrange("p m t (j r) -> p m j r t", r=2)
    nc.vector.tensor_scalar_mul(out=partner[:, :, :, 0, :], in0=pairs[:, :, :, 1, :], scalar1=-1.0)
    nc.vector.tensor_copy(out=partner[:, :, :, 1, :], in_=pairs[:, :, :, 0, :])
    nc.vector.tensor_copy(out=grouped[:, ROT:W_COLS, :], in_=raw[:, 2].rearrange("p t c -> p c t"))

    codes = consts.tile([P, W_COLS], U32, align_bytes=64)
    scales = consts.tile([P, W_COLS], U8, align_bytes=64)
    for cols in (slice(0, ROT), slice(ROT, W_COLS)):
        nc.vector.quantize_mx(
            out=codes[:, cols].bitcast(FP8X4),
            scales=scales[:, cols],
            in_=grouped[:, cols, :].rearrange("p c t -> p (c t)"),
        )
    return codes, scales


def tile_flexattentionblock_pa_t_kernel(tc, x, attn_norm_w, wq, wk, wv, out_0, out_1, out_2):
    nc = tc.nc
    n_groups = BATCH * GROUPS
    with ExitStack() as ctx:
        consts = ctx.enter_context(tc.tile_pool(name="consts", bufs=1))
        setup = ctx.enter_context(tc.tile_pool(name="setup", bufs=1))
        resident = ctx.enter_context(tc.tile_pool(name="resident", bufs=1))
        stream = ctx.enter_context(tc.tile_pool(name="stream", bufs=3))
        per_tile = ctx.enter_context(tc.tile_pool(name="per_tile", bufs=GROUP))
        psum_gain = ctx.enter_context(tc.psum_pool(name="psum_gain", bufs=1))
        psum_t = ctx.enter_context(tc.psum_pool(name="psum_t", bufs=2))
        psum_rot = ctx.enter_context(tc.psum_pool(name="psum_rot", bufs=GROUP))
        psum_v = ctx.enter_context(tc.psum_pool(name="psum_v", bufs=1))
        ctx.enter_context(tc.manual_schedule())

        zero_col = setup.tile([P, 1], F32)
        nc.vector.memset(zero_col[:], 0.0)
        nc.scalar.activation(out=zero_col[:], in_=zero_col[:], func=ACT.Sin)

        gain_row = setup.tile([P, DIM], BF16)
        nc.vector.memset(gain_row[:], 0.0)
        x_groups = []
        for b in range(BATCH):
            tokens = x[b].rearrange("(p i) k -> p i k", i=TILES)
            for g in range(GROUPS):
                x_sb = resident.tile([P, GROUP, DIM], BF16, name="x_%d_%d" % (b, g))
                nc.sync.dma_start(out=x_sb[:], in_=tokens[:, g * GROUP : (g + 1) * GROUP, :])
                x_groups.append(x_sb)
                if b == 0 and g == 0:
                    nc.sync.dma_start(
                        out=gain_row[0:1, :], in_=attn_norm_w.rearrange("(o k) -> o k", o=1)
                    )
                    w_raw = load_weights(nc, setup, wq, wk, wv)

        turns = rotation_turns(nc, setup)
        identity = consts.tile([P, P], F32)
        masks.make_identity(nc, identity[:])
        eps_col = consts.tile([P, 1], F32)
        nc.vector.memset(eps_col[:], EPS)

        ones = setup.tile([P, P], BF16)
        nc.vector.memset(ones[:], 1.0)
        gain = psum_gain.tile([P, DIM], F32)
        nc.tensor.matmul(out=gain[:], lhsT=ones[:], rhs=gain_row[:], start=True, stop=True)
        w_codes, w_scales = quantise_weights(nc, consts, setup, w_raw)

        squares_of, root_of, rstd_of, h_of, grouped_of, codes_of = {}, {}, {}, {}, {}, {}
        v_bank_of, rot_banks_of = {}, {}

        def sum_squares(n, half):
            if half == 0:
                squares = stream.tile([P, GROUP], F32)
                squares_of[n] = squares
            for t in (2 * half, 2 * half + 1):
                unread = per_tile.tile([P, DIM], BF16)
                nc.scalar.activation(
                    out=unread[:], in_=x_groups[n][:, t, :], func=ACT.Square,
                    accum_out=squares_of[n][:, t : t + 1],
                )

        def root_mean_square(n):
            root = stream.tile([P, GROUP], F32)
            nc.scalar.activation(
                out=root[:], in_=squares_of[n][:], func=ACT.Sqrt, scale=1.0 / DIM, bias=eps_col[:]
            )
            root_of[n] = root

        def reciprocal_root(n):
            rstd = stream.tile([P, GROUP], F32)
            nc.vector.reciprocal(out=rstd[:], in_=root_of[n][:])
            rstd_of[n] = rstd

        def scale_and_turn(n, half):
            if half == 0:
                h = stream.tile([P, GROUP, DIM], BF16)
                grouped = stream.tile([P, GROUP * P * PACK], BF16, align_bytes=64)
                h_of[n], grouped_of[n] = h, grouped
            h = h_of[n]
            for t in (2 * half, 2 * half + 1):
                nc.vector.scalar_tensor_tensor(
                    out=h[:, t, :], in0=x_groups[n][:, t, :], scalar=rstd_of[n][:, t : t + 1],
                    in1=gain[:], op0=ALU.mult, op1=ALU.mult,
                )
            turned = psum_t.tile([P, 2, 2 * P], F32)
            for s in range(2):
                words = h[:, 2 * half + s, :].bitcast(F32)
                for u in range(2):
                    nc.tensor.transpose(
                        out=turned[:, u, s * P : (s + 1) * P],
                        in_=words[:, u * P : (u + 1) * P],
                        identity=identity[:],
                    )
            grouped_words = grouped_of[n][:].bitcast(F32).rearrange("p (r u) -> p r u", u=2)
            nc.scalar.copy(
                out=grouped_words[:, half * 2 * P : (half + 1) * 2 * P, :],
                in_=turned[:].rearrange("p u r -> p r u"),
            )

        def quantise(n):
            h_codes = stream.tile([P, GROUP * P], U32, align_bytes=64)
            h_scales = stream.tile([P, GROUP * P], U8, align_bytes=64)
            nc.vector.quantize_mx(
                out=h_codes[:].bitcast(FP8X4), scales=h_scales[:], in_=grouped_of[n][:]
            )
            codes_of[n] = (h_codes, h_scales)

        def project_v(n):
            h_codes, h_scales = codes_of[n]
            v_ps = psum_v.tile([P, GROUP, QD], F32)
            for t in range(GROUP):
                cols = slice(t * P, (t + 1) * P)
                nc.tensor.matmul_mx(
                    out=v_ps[:, t, :],
                    lhsT=h_codes[:, cols].bitcast(FP8X4), lhsT_scale=h_scales[:, cols],
                    rhs=w_codes[:, ROT:W_COLS].bitcast(FP8X4), rhs_scale=w_scales[:, ROT:W_COLS],
                    start=True, stop=True,
                )
            v_bank_of[n] = v_ps

        def project_rot(n):
            h_codes, h_scales = codes_of[n]
            rot_banks = []
            for t in range(GROUP):
                cols = slice(t * P, (t + 1) * P)
                rot_ps = psum_rot.tile([P, ROT], F32)
                nc.tensor.matmul_mx(
                    out=rot_ps[:],
                    lhsT=h_codes[:, cols].bitcast(FP8X4), lhsT_scale=h_scales[:, cols],
                    rhs=w_codes[:, 0:ROT].bitcast(FP8X4), rhs_scale=w_scales[:, 0:ROT],
                    start=True, stop=True,
                )
                rot_banks.append(rot_ps)
            rot_banks_of[n] = rot_banks

        def store(n, dram, sb):
            b, g = divmod(n, GROUPS)
            rows = dram[b].rearrange("h (p i) d -> p h i d", i=TILES)
            nc.sync.dma_start(out=rows[:, :, g * GROUP : (g + 1) * GROUP, :], in_=sb)

        def store_v(n):
            v_sb = stream.tile([P, HEADS, GROUP, HEAD_DIM], F32)
            nc.scalar.copy(
                out=v_sb[:], in_=v_bank_of[n][:].rearrange("p t (h d) -> p h t d", h=HEADS)
            )
            store(n, out_2, v_sb[:])

        def rotate_and_store(n):
            first_tile = (n % GROUPS) * GROUP
            rotated = stream.tile([P, 2 * HEADS, GROUP, HEAD_DIM], F32)
            for t in range(GROUP):
                products = per_tile.tile([P, 2, 2 * HEADS, HEAD_DIM], F32)
                nc.vector.tensor_tensor(
                    out=products[:],
                    in0=rot_banks_of[n][t][:].rearrange("p (c r d) -> p c r d", c=2, r=2 * HEADS),
                    in1=table[:, first_tile + t].unsqueeze(2).to_broadcast(
                        [P, 2, 2 * HEADS, HEAD_DIM]
                    ),
                    op=ALU.mult,
                )
                nc.gpsimd.tensor_tensor(
                    out=rotated[:, :, t, :], in0=products[:, 0], in1=products[:, 1], op=ALU.add
                )
            store(n, out_0, rotated[:, 0:HEADS])
            store(n, out_1, rotated[:, HEADS:])

        sum_squares(0, 0)
        sum_squares(0, 1)
        table = rotation_table(nc, consts, setup, turns)
        root_mean_square(0)
        reciprocal_root(0)
        sum_squares(1, 0)
        sum_squares(1, 1)
        root_mean_square(1)

        for n in range(n_groups + 2):
            ahead, behind, last = n + 2, n - 1, n - 2
            if ahead < n_groups:
                sum_squares(ahead, 0)
            if n < n_groups:
                scale_and_turn(n, 0)
            if 0 <= behind < n_groups:
                quantise(behind)
            if ahead < n_groups:
                sum_squares(ahead, 1)
                root_mean_square(ahead)
            if n < n_groups:
                scale_and_turn(n, 1)
            if n + 1 < n_groups:
                reciprocal_root(n + 1)
            if 0 <= behind < n_groups:
                project_v(behind)
                store_v(behind)
            if last >= 0:
                rotate_and_store(last)
            if 0 <= behind < n_groups:
                project_rot(behind)
